import numpy as np
import ml_dtypes

BF16 = ml_dtypes.bfloat16


def bf(x):
    return np.asarray(x, np.float32).astype(BF16)


def f32(x):
    return np.asarray(x, np.float32)


def f64(x):
    return np.asarray(x).astype(np.float64)


def striped(idx):
    return np.tile(idx.reshape(-1, 16).T, (8, 1))


S, D, M, E, N = 256, 128, 512, 128, 128
TERMS = 150


def erf_series(a):
    a = np.asarray(a, np.float64)
    c = np.clip(a, -6.0, 6.0)
    term = c.copy()
    tot = c.copy()
    for n in range(TERMS - 1):
        term = term * (2.0 * c * c) / (2.0 * n + 3.0)
        tot = tot + term
    val = 2.0 / np.sqrt(np.pi) * np.exp(-c * c) * tot
    return np.where(np.abs(a) > 6.0, np.sign(a), val)


def gelu_erf(v):
    return 0.5 * v * (1.0 + erf_series(v / np.sqrt(2.0)))


def setup_inputs():
    return {"table": bf(np.random.standard_normal((S, D))), "w1x": bf(np.random.standard_normal((D, M)) / np.sqrt(2.0 * D)), "w1k": bf(np.random.standard_normal((D, M)) / np.sqrt(2.0 * D)), "know": bf(np.random.standard_normal((D, 1))), "b1": f32(0.1 * np.random.standard_normal((M, 1))), "w2": bf(np.random.standard_normal((M, E)) / np.sqrt(M)), "b2": f32(0.1 * np.random.standard_normal((E, 1))), "offs": striped(np.random.permutation(S)[:N])}


def reference(table, w1x, w1k, know, b1, w2, b2, offs):
    idx = offs[:16].T.reshape(-1)
    pre = f64(w1x).T @ f64(table)[idx].T + f64(w1k).T @ f64(know) + f64(b1)
    g = gelu_erf(pre)
    return np.tanh(f64(w2).T @ g + f64(b2))

@@ -1,0 +1,67 @@
+import concourse.mybir as mybir
+from concourse.masks import make_identity
+
+P = 128
+S, D, M, E, N = 256, 128, 512, 128, 128
+S_BLOCKS = S // P
+M_BLOCKS = M // P
+FLOPS = 2 * D * M * N + 2 * D * M + 2 * M * E * N
+
+BF16, F32, U16 = mybir.dt.bfloat16, mybir.dt.float32, mybir.dt.uint16
+GELU = mybir.ActivationFunctionType.Gelu
+TANH = mybir.ActivationFunctionType.Tanh
+
+
+def tile_universalknowledgeintegrator_kernel(tc, table, w1x, w1k, know, b1, w2, b2, offs, out):
+    nc = tc.nc
+    with (
+        tc.tile_pool(name="held", bufs=1) as held,
+        tc.psum_pool(name="banks", bufs=1) as banks,
+    ):
+        offsets = held.tile([P, N // 16], U16, name="offsets")
+        nc.sync.dma_start(offsets[:], offs)
+        rows = [held.tile([P, D], BF16, name=f"rows{s}") for s in range(S_BLOCKS)]
+        nc.sync.dma_start(rows[0][:], table[0:P, :])
+        nc.scalar.dma_start(rows[1][:], table[P : 2 * P, :])
+        know_sb = held.tile([D, 1], BF16, name="know_sb")
+        nc.scalar.dma_start(know_sb[:], know)
+        w1k_sb = held.tile([D, M], BF16, name="w1k_sb")
+        nc.sync.dma_start(w1k_sb[:], w1k)
+        w1x_sb = held.tile([D, M], BF16, name="w1x_sb")
+        nc.scalar.dma_start(w1x_sb[:], w1x)
+        b1_sb = held.tile([P, M_BLOCKS], F32, name="b1_sb")
+        with nc.allow_non_contiguous_dma(reason="512 floats, one to a partition and block"):
+            nc.sync.dma_start(b1_sb[:], b1.rearrange("(c p) o -> p (c o)", p=P))
+        w2_sb = held.tile([P, M_BLOCKS, E], BF16, name="w2_sb")
+        nc.scalar.dma_start(w2_sb[:], w2.rearrange("(c p) e -> p c e", p=P))
+        b2_sb = held.tile([E, 1], F32, name="b2_sb")
+        nc.sync.dma_start(b2_sb[:], b2)
+
+        identity = held.tile([P, P], BF16, name="identity")
+        make_identity(nc, identity[:])
+        flipped = banks.tile([D, S], BF16, name="flipped")
+        for s in range(S_BLOCKS):
+            nc.tensor.transpose(flipped[:, s * P : (s + 1) * P], rows[s][:], identity[:])
+        window = held.tile([D, S], BF16, name="window")
+        nc.vector.tensor_copy(window[:], flipped[:])
+
+        pre = [banks.tile([P, N], F32, name=f"pre{c}") for c in range(M_BLOCKS)]
+        for c in range(M_BLOCKS):
+            nc.tensor.matmul(
+                pre[c][:], w1k_sb[:, c * P : (c + 1) * P], know_sb[:, 0:1].to_broadcast([D, N]),
+                start=True, stop=False,
+            )
+
+        total = banks.tile([E, N], F32, name="total")
+        for c in range(M_BLOCKS):
+            nc.tensor.matmul(
+                pre[c][:], w1x_sb[:, c * P : (c + 1) * P], window[:].indirect(offsets[:]),
+                start=False, stop=True,
+            )
+            g = held.tile([P, N], BF16, name=f"g{c}")
+            nc.scalar.activation(g[:], pre[c][:], GELU, bias=b1_sb[:, c : c + 1])
+            nc.tensor.matmul(total[:], w2_sb[:, c, :], g[:], start=(c == 0), stop=(c == M_BLOCKS - 1))
+
+        result = held.tile([E, N], F32, name="result")
+        nc.scalar.activation(result[:], total[:], TANH, bias=b2_sb[:, 0:1])
+        nc.sync.dma_start(out, result[:])

@@ -37,6 +37,10 @@ def tile_universalknowledgeintegrator_kernel(tc, table, w1x, w1k, know, b1, w2, 
         b2_sb = held.tile([E, 1], F32, name="b2_sb")
         nc.sync.dma_start(b2_sb[:], b2)
 
+        warm = held.tile([P, 1], F32, name="warm")
+        nc.vector.memset(warm[:], 0.0)
+        nc.scalar.activation(warm[:], warm[:], GELU)
+
         identity = held.tile([P, P], BF16, name="identity")
         make_identity(nc, identity[:])
         flipped = banks.tile([D, S], BF16, name="flipped")
@@ -52,12 +56,14 @@ def tile_universalknowledgeintegrator_kernel(tc, table, w1x, w1k, know, b1, w2, 
                 start=True, stop=False,
             )
 
-        total = banks.tile([E, N], F32, name="total")
         for c in range(M_BLOCKS):
             nc.tensor.matmul(
                 pre[c][:], w1x_sb[:, c * P : (c + 1) * P], window[:].indirect(offsets[:]),
                 start=False, stop=True,
             )
+
+        total = banks.tile([E, N], F32, name="total")
+        for c in range(M_BLOCKS):
             g = held.tile([P, N], BF16, name=f"g{c}")
             nc.scalar.activation(g[:], pre[c][:], GELU, bias=b1_sb[:, c : c + 1])
             nc.tensor.matmul(total[:], w2_sb[:, c, :], g[:], start=(c == 0), stop=(c == M_BLOCKS - 1))

@@ -37,10 +37,6 @@ def tile_universalknowledgeintegrator_kernel(tc, table, w1x, w1k, know, b1, w2, 
         b2_sb = held.tile([E, 1], F32, name="b2_sb")
         nc.sync.dma_start(b2_sb[:], b2)
 
-        warm = held.tile([P, 1], F32, name="warm")
-        nc.vector.memset(warm[:], 0.0)
-        nc.scalar.activation(warm[:], warm[:], GELU)
-
         identity = held.tile([P, P], BF16, name="identity")
         make_identity(nc, identity[:])
         flipped = banks.tile([D, S], BF16, name="flipped")

@@ -5,6 +5,8 @@ P = 128
 S, D, M, E, N = 256, 128, 512, 128, 128
 S_BLOCKS = S // P
 M_BLOCKS = M // P
+WARM_COLUMNS = 512
+WARM_MATMULS = 5
 FLOPS = 2 * D * M * N + 2 * D * M + 2 * M * E * N
 
 BF16, F32, U16 = mybir.dt.bfloat16, mybir.dt.float32, mybir.dt.uint16
@@ -36,6 +38,16 @@ def tile_universalknowledgeintegrator_kernel(tc, table, w1x, w1k, know, b1, w2, 
         nc.scalar.dma_start(w2_sb[:], w2.rearrange("(c p) e -> p c e", p=P))
         b2_sb = held.tile([E, 1], F32, name="b2_sb")
         nc.sync.dma_start(b2_sb[:], b2)
+
+        warm = held.tile([P, 1], F32, name="warm")
+        nc.vector.memset(warm[:], 0.0)
+        nc.scalar.activation(warm[:], warm[:], GELU)
+
+        zeros = held.tile([P, WARM_COLUMNS], BF16, name="zeros")
+        nc.vector.memset(zeros[:], 0.0)
+        unread = banks.tile([P, WARM_COLUMNS], F32, name="unread")
+        for w in range(WARM_MATMULS):
+            nc.tensor.matmul(unread[:], zeros[:, 0:P], zeros[:], start=True, stop=True)
 
         identity = held.tile([P, P], BF16, name="identity")
         make_identity(nc, identity[:])

@@ -5,8 +5,7 @@ P = 128
 S, D, M, E, N = 256, 128, 512, 128, 128
 S_BLOCKS = S // P
 M_BLOCKS = M // P
-WARM_COLUMNS = 512
-WARM_MATMULS = 5
+WARM_MATMULS = 16
 FLOPS = 2 * D * M * N + 2 * D * M + 2 * M * E * N
 
 BF16, F32, U16 = mybir.dt.bfloat16, mybir.dt.float32, mybir.dt.uint16
@@ -39,15 +38,15 @@ def tile_universalknowledgeintegrator_kernel(tc, table, w1x, w1k, know, b1, w2, 
         b2_sb = held.tile([E, 1], F32, name="b2_sb")
         nc.sync.dma_start(b2_sb[:], b2)
 
+        zeros = held.tile([P, P], BF16, name="zeros")
+        nc.vector.memset(zeros[:], 0.0)
+        unread = banks.tile([P, P], F32, name="unread")
+        for w in range(WARM_MATMULS):
+            nc.tensor.matmul(unread[:], zeros[:], zeros[:], start=True, stop=True)
+
         warm = held.tile([P, 1], F32, name="warm")
         nc.vector.memset(warm[:], 0.0)
         nc.scalar.activation(warm[:], warm[:], GELU)
-
-        zeros = held.tile([P, WARM_COLUMNS], BF16, name="zeros")
-        nc.vector.memset(zeros[:], 0.0)
-        unread = banks.tile([P, WARM_COLUMNS], F32, name="unread")
-        for w in range(WARM_MATMULS):
-            nc.tensor.matmul(unread[:], zeros[:, 0:P], zeros[:], start=True, stop=True)
 
         identity = held.tile([P, P], BF16, name="identity")
         make_identity(nc, identity[:])

@@ -19,8 +19,6 @@ def tile_universalknowledgeintegrator_kernel(tc, table, w1x, w1k, know, b1, w2, 
         tc.tile_pool(name="held", bufs=1) as held,
         tc.psum_pool(name="banks", bufs=1) as banks,
     ):
-        offsets = held.tile([P, N // 16], U16, name="offsets")
-        nc.sync.dma_start(offsets[:], offs)
         rows = [held.tile([P, D], BF16, name=f"rows{s}") for s in range(S_BLOCKS)]
         nc.sync.dma_start(rows[0][:], table[0:P, :])
         nc.scalar.dma_start(rows[1][:], table[P : 2 * P, :])
@@ -28,6 +26,8 @@ def tile_universalknowledgeintegrator_kernel(tc, table, w1x, w1k, know, b1, w2, 
         nc.scalar.dma_start(know_sb[:], know)
         w1k_sb = held.tile([D, M], BF16, name="w1k_sb")
         nc.sync.dma_start(w1k_sb[:], w1k)
+        offsets = held.tile([P, N // 16], U16, name="offsets")
+        nc.sync.dma_start(offsets[:], offs)
         w1x_sb = held.tile([D, M], BF16, name="w1x_sb")
         nc.scalar.dma_start(w1x_sb[:], w1x)
         b1_sb = held.tile([P, M_BLOCKS], F32, name="b1_sb")
@@ -50,11 +50,12 @@ def tile_universalknowledgeintegrator_kernel(tc, table, w1x, w1k, know, b1, w2, 
 
         identity = held.tile([P, P], BF16, name="identity")
         make_identity(nc, identity[:])
-        flipped = banks.tile([D, S], BF16, name="flipped")
-        for s in range(S_BLOCKS):
-            nc.tensor.transpose(flipped[:, s * P : (s + 1) * P], rows[s][:], identity[:])
         window = held.tile([D, S], BF16, name="window")
-        nc.vector.tensor_copy(window[:], flipped[:])
+        flipped = [banks.tile([D, P], BF16, name=f"flipped{s}") for s in range(S_BLOCKS)]
+        for s in range(S_BLOCKS):
+            nc.tensor.transpose(flipped[s][:], rows[s][:], identity[:])
+        nc.vector.tensor_copy(window[:, 0:P], flipped[0][:])
+        nc.scalar.copy(window[:, P : 2 * P], flipped[1][:])
 
         pre = [banks.tile([P, N], F32, name=f"pre{c}") for c in range(M_BLOCKS)]
         for c in range(M_BLOCKS):
@@ -77,4 +78,4 @@ def tile_universalknowledgeintegrator_kernel(tc, table, w1x, w1k, know, b1, w2, 
 
         result = held.tile([E, N], F32, name="result")
         nc.scalar.activation(result[:], total[:], TANH, bias=b2_sb[:, 0:1])
-        nc.sync.dma_start(out, result[:])
+        nc.scalar.dma_start(out, result[:])

@@ -19,20 +19,19 @@ def tile_universalknowledgeintegrator_kernel(tc, table, w1x, w1k, know, b1, w2, 
         tc.tile_pool(name="held", bufs=1) as held,
         tc.psum_pool(name="banks", bufs=1) as banks,
     ):
-        rows = [held.tile([P, D], BF16, name=f"rows{s}") for s in range(S_BLOCKS)]
-        nc.sync.dma_start(rows[0][:], table[0:P, :])
-        nc.scalar.dma_start(rows[1][:], table[P : 2 * P, :])
+        rows = held.tile([P, S_BLOCKS, D], BF16, name="rows")
+        nc.sync.dma_start(rows[:], table.rearrange("(s p) d -> p s d", p=P))
         know_sb = held.tile([D, 1], BF16, name="know_sb")
         nc.scalar.dma_start(know_sb[:], know)
         w1k_sb = held.tile([D, M], BF16, name="w1k_sb")
         nc.sync.dma_start(w1k_sb[:], w1k)
-        offsets = held.tile([P, N // 16], U16, name="offsets")
-        nc.sync.dma_start(offsets[:], offs)
         w1x_sb = held.tile([D, M], BF16, name="w1x_sb")
         nc.scalar.dma_start(w1x_sb[:], w1x)
+        offsets = held.tile([P, N // 16], U16, name="offsets")
+        nc.sync.dma_start(offsets[:], offs)
         b1_sb = held.tile([P, M_BLOCKS], F32, name="b1_sb")
         with nc.allow_non_contiguous_dma(reason="512 floats, one to a partition and block"):
-            nc.sync.dma_start(b1_sb[:], b1.rearrange("(c p) o -> p (c o)", p=P))
+            nc.scalar.dma_start(b1_sb[:], b1.rearrange("(c p) o -> p (c o)", p=P))
         w2_sb = held.tile([P, M_BLOCKS, E], BF16, name="w2_sb")
         nc.scalar.dma_start(w2_sb[:], w2.rearrange("(c p) e -> p c e", p=P))
         b2_sb = held.tile([E, 1], F32, name="b2_sb")
@@ -50,12 +49,11 @@ def tile_universalknowledgeintegrator_kernel(tc, table, w1x, w1k, know, b1, w2, 
 
         identity = held.tile([P, P], BF16, name="identity")
         make_identity(nc, identity[:])
-        window = held.tile([D, S], BF16, name="window")
-        flipped = [banks.tile([D, P], BF16, name=f"flipped{s}") for s in range(S_BLOCKS)]
+        flipped = banks.tile([D, S], BF16, name="flipped")
         for s in range(S_BLOCKS):
-            nc.tensor.transpose(flipped[s][:], rows[s][:], identity[:])
-        nc.vector.tensor_copy(window[:, 0:P], flipped[0][:])
-        nc.scalar.copy(window[:, P : 2 * P], flipped[1][:])
+            nc.tensor.transpose(flipped[:, s * P : (s + 1) * P], rows[:, s, :], identity[:])
+        window = held.tile([D, S], BF16, name="window")
+        nc.vector.tensor_copy(window[:], flipped[:])
 
         pre = [banks.tile([P, N], F32, name=f"pre{c}") for c in range(M_BLOCKS)]
         for c in range(M_BLOCKS):
@@ -78,4 +76,4 @@ def tile_universalknowledgeintegrator_kernel(tc, table, w1x, w1k, know, b1, w2, 
 
         result = held.tile([E, N], F32, name="result")
         nc.scalar.activation(result[:], total[:], TANH, bias=b2_sb[:, 0:1])
-        nc.scalar.dma_start(out, result[:])
+        nc.sync.dma_start(out, result[:])

@@ -5,6 +5,7 @@ P = 128
 S, D, M, E, N = 256, 128, 512, 128, 128
 S_BLOCKS = S // P
 M_BLOCKS = M // P
+BIAS_ROWS = M_BLOCKS + 1
 WARM_MATMULS = 16
 FLOPS = 2 * D * M * N + 2 * D * M + 2 * M * E * N
 
@@ -29,13 +30,12 @@ def tile_universalknowledgeintegrator_kernel(tc, table, w1x, w1k, know, b1, w2, 
         nc.scalar.dma_start(w1x_sb[:], w1x)
         offsets = held.tile([P, N // 16], U16, name="offsets")
         nc.sync.dma_start(offsets[:], offs)
-        b1_sb = held.tile([P, M_BLOCKS], F32, name="b1_sb")
-        with nc.allow_non_contiguous_dma(reason="512 floats, one to a partition and block"):
-            nc.scalar.dma_start(b1_sb[:], b1.rearrange("(c p) o -> p (c o)", p=P))
+        bias_rows = held.tile([P, P], F32, name="bias_rows")
+        nc.vector.memset(bias_rows[:], 0.0)
+        nc.scalar.dma_start(bias_rows[0:M_BLOCKS, :], b1.rearrange("(c p) o -> c (p o)", p=P))
         w2_sb = held.tile([P, M_BLOCKS, E], BF16, name="w2_sb")
         nc.scalar.dma_start(w2_sb[:], w2.rearrange("(c p) e -> p c e", p=P))
-        b2_sb = held.tile([E, 1], F32, name="b2_sb")
-        nc.sync.dma_start(b2_sb[:], b2)
+        nc.sync.dma_start(bias_rows[M_BLOCKS:BIAS_ROWS, :], b2.rearrange("e o -> o e"))
 
         zeros = held.tile([P, P], BF16, name="zeros")
         nc.vector.memset(zeros[:], 0.0)
@@ -49,11 +49,18 @@ def tile_universalknowledgeintegrator_kernel(tc, table, w1x, w1k, know, b1, w2, 
 
         identity = held.tile([P, P], BF16, name="identity")
         make_identity(nc, identity[:])
+        pick = held.tile([P, BIAS_ROWS], F32, name="pick")
+        nc.vector.tensor_copy(pick[:], identity[:, 0:BIAS_ROWS])
         flipped = banks.tile([D, S], BF16, name="flipped")
         for s in range(S_BLOCKS):
             nc.tensor.transpose(flipped[:, s * P : (s + 1) * P], rows[:, s, :], identity[:])
         window = held.tile([D, S], BF16, name="window")
         nc.vector.tensor_copy(window[:], flipped[:])
+
+        bias_cols = banks.tile([P, BIAS_ROWS], F32, name="bias_cols")
+        nc.tensor.matmul(bias_cols[:], bias_rows[:], pick[:], start=True, stop=True)
+        biases = held.tile([P, BIAS_ROWS], F32, name="biases")
+        nc.vector.tensor_copy(biases[:], bias_cols[:])
 
         pre = [banks.tile([P, N], F32, name=f"pre{c}") for c in range(M_BLOCKS)]
         for c in range(M_BLOCKS):
@@ -71,9 +78,9 @@ def tile_universalknowledgeintegrator_kernel(tc, table, w1x, w1k, know, b1, w2, 
         total = banks.tile([E, N], F32, name="total")
         for c in range(M_BLOCKS):
             g = held.tile([P, N], BF16, name=f"g{c}")
-            nc.scalar.activation(g[:], pre[c][:], GELU, bias=b1_sb[:, c : c + 1])
+            nc.scalar.activation(g[:], pre[c][:], GELU, bias=biases[:, c : c + 1])
             nc.tensor.matmul(total[:], w2_sb[:, c, :], g[:], start=(c == 0), stop=(c == M_BLOCKS - 1))
 
         result = held.tile([E, N], F32, name="result")
-        nc.scalar.activation(result[:], total[:], TANH, bias=b2_sb[:, 0:1])
+        nc.scalar.activation(result[:], total[:], TANH, bias=biases[:, M_BLOCKS:BIAS_ROWS])
         nc.sync.dma_start(out, result[:])

@@ -57,30 +57,29 @@ def tile_universalknowledgeintegrator_kernel(tc, table, w1x, w1k, know, b1, w2, 
         window = held.tile([D, S], BF16, name="window")
         nc.vector.tensor_copy(window[:], flipped[:])
 
-        bias_cols = banks.tile([P, BIAS_ROWS], F32, name="bias_cols")
-        nc.tensor.matmul(bias_cols[:], bias_rows[:], pick[:], start=True, stop=True)
-        biases = held.tile([P, BIAS_ROWS], F32, name="biases")
-        nc.vector.tensor_copy(biases[:], bias_cols[:])
+        shift_cols = banks.tile([P, BIAS_ROWS], F32, name="shift_cols")
+        nc.tensor.matmul(shift_cols[:], bias_rows[:], pick[:], start=True, stop=False)
+        for c in range(M_BLOCKS):
+            nc.tensor.matmul(
+                shift_cols[:, c : c + 1], w1k_sb[:, c * P : (c + 1) * P], know_sb[:, 0:1],
+                start=False, stop=(c == M_BLOCKS - 1),
+            )
+        shifts = held.tile([P, BIAS_ROWS], F32, name="shifts")
+        nc.vector.tensor_copy(shifts[:], shift_cols[:])
 
         pre = [banks.tile([P, N], F32, name=f"pre{c}") for c in range(M_BLOCKS)]
         for c in range(M_BLOCKS):
             nc.tensor.matmul(
-                pre[c][:], w1k_sb[:, c * P : (c + 1) * P], know_sb[:, 0:1].to_broadcast([D, N]),
-                start=True, stop=False,
-            )
-
-        for c in range(M_BLOCKS):
-            nc.tensor.matmul(
                 pre[c][:], w1x_sb[:, c * P : (c + 1) * P], window[:].indirect(offsets[:]),
-                start=False, stop=True,
+                start=True, stop=True,
             )
 
         total = banks.tile([E, N], F32, name="total")
         for c in range(M_BLOCKS):
             g = held.tile([P, N], BF16, name=f"g{c}")
-            nc.scalar.activation(g[:], pre[c][:], GELU, bias=biases[:, c : c + 1])
+            nc.scalar.activation(g[:], pre[c][:], GELU, bias=shifts[:, c : c + 1])
             nc.tensor.matmul(total[:], w2_sb[:, c, :], g[:], start=(c == 0), stop=(c == M_BLOCKS - 1))
 
         result = held.tile([E, N], F32, name="result")
-        nc.scalar.activation(result[:], total[:], TANH, bias=biases[:, M_BLOCKS:BIAS_ROWS])
+        nc.scalar.activation(result[:], total[:], TANH, bias=shifts[:, M_BLOCKS:BIAS_ROWS])
         nc.sync.dma_start(out, result[:])

@@ -22,14 +22,14 @@ def tile_universalknowledgeintegrator_kernel(tc, table, w1x, w1k, know, b1, w2, 
     ):
         rows = held.tile([P, S_BLOCKS, D], BF16, name="rows")
         nc.sync.dma_start(rows[:], table.rearrange("(s p) d -> p s d", p=P))
+        offsets = held.tile([P, N // 16], U16, name="offsets")
+        nc.sync.dma_start(offsets[:], offs)
         know_sb = held.tile([D, 1], BF16, name="know_sb")
         nc.scalar.dma_start(know_sb[:], know)
         w1k_sb = held.tile([D, M], BF16, name="w1k_sb")
         nc.sync.dma_start(w1k_sb[:], w1k)
         w1x_sb = held.tile([D, M], BF16, name="w1x_sb")
         nc.scalar.dma_start(w1x_sb[:], w1x)
-        offsets = held.tile([P, N // 16], U16, name="offsets")
-        nc.sync.dma_start(offsets[:], offs)
         bias_rows = held.tile([P, P], F32, name="bias_rows")
         nc.vector.memset(bias_rows[:], 0.0)
         nc.scalar.dma_start(bias_rows[0:M_BLOCKS, :], b1.rearrange("(c p) o -> c (p o)", p=P))

@@ -5,7 +5,6 @@ P = 128
 S, D, M, E, N = 256, 128, 512, 128, 128
 S_BLOCKS = S // P
 M_BLOCKS = M // P
-BIAS_ROWS = M_BLOCKS + 1
 WARM_MATMULS = 16
 FLOPS = 2 * D * M * N + 2 * D * M + 2 * M * E * N
 
@@ -24,18 +23,19 @@ def tile_universalknowledgeintegrator_kernel(tc, table, w1x, w1k, know, b1, w2, 
         nc.sync.dma_start(rows[:], table.rearrange("(s p) d -> p s d", p=P))
         offsets = held.tile([P, N // 16], U16, name="offsets")
         nc.sync.dma_start(offsets[:], offs)
+        bias_rows = held.tile([P, P], F32, name="bias_rows")
+        nc.vector.memset(bias_rows[:], 0.0)
+        nc.scalar.dma_start(bias_rows[0:M_BLOCKS, :], b1.rearrange("(c p) o -> c (p o)", p=P))
         know_sb = held.tile([D, 1], BF16, name="know_sb")
         nc.scalar.dma_start(know_sb[:], know)
         w1k_sb = held.tile([D, M], BF16, name="w1k_sb")
         nc.sync.dma_start(w1k_sb[:], w1k)
         w1x_sb = held.tile([D, M], BF16, name="w1x_sb")
         nc.scalar.dma_start(w1x_sb[:], w1x)
-        bias_rows = held.tile([P, P], F32, name="bias_rows")
-        nc.vector.memset(bias_rows[:], 0.0)
-        nc.scalar.dma_start(bias_rows[0:M_BLOCKS, :], b1.rearrange("(c p) o -> c (p o)", p=P))
         w2_sb = held.tile([P, M_BLOCKS, E], BF16, name="w2_sb")
         nc.scalar.dma_start(w2_sb[:], w2.rearrange("(c p) e -> p c e", p=P))
-        nc.sync.dma_start(bias_rows[M_BLOCKS:BIAS_ROWS, :], b2.rearrange("e o -> o e"))
+        b2_sb = held.tile([E, 1], F32, name="b2_sb")
+        nc.sync.dma_start(b2_sb[:], b2)
 
         zeros = held.tile([P, P], BF16, name="zeros")
         nc.vector.memset(zeros[:], 0.0)
@@ -49,22 +49,22 @@ def tile_universalknowledgeintegrator_kernel(tc, table, w1x, w1k, know, b1, w2, 
 
         identity = held.tile([P, P], BF16, name="identity")
         make_identity(nc, identity[:])
-        pick = held.tile([P, BIAS_ROWS], F32, name="pick")
-        nc.vector.tensor_copy(pick[:], identity[:, 0:BIAS_ROWS])
+        pick = held.tile([P, M_BLOCKS], F32, name="pick")
+        nc.vector.tensor_copy(pick[:], identity[:, 0:M_BLOCKS])
         flipped = banks.tile([D, S], BF16, name="flipped")
         for s in range(S_BLOCKS):
             nc.tensor.transpose(flipped[:, s * P : (s + 1) * P], rows[:, s, :], identity[:])
         window = held.tile([D, S], BF16, name="window")
         nc.vector.tensor_copy(window[:], flipped[:])
 
-        shift_cols = banks.tile([P, BIAS_ROWS], F32, name="shift_cols")
+        shift_cols = banks.tile([P, M_BLOCKS], F32, name="shift_cols")
         nc.tensor.matmul(shift_cols[:], bias_rows[:], pick[:], start=True, stop=False)
         for c in range(M_BLOCKS):
             nc.tensor.matmul(
                 shift_cols[:, c : c + 1], w1k_sb[:, c * P : (c + 1) * P], know_sb[:, 0:1],
                 start=False, stop=(c == M_BLOCKS - 1),
             )
-        shifts = held.tile([P, BIAS_ROWS], F32, name="shifts")
+        shifts = held.tile([P, M_BLOCKS], F32, name="shifts")
         nc.vector.tensor_copy(shifts[:], shift_cols[:])
 
         pre = [banks.tile([P, N], F32, name=f"pre{c}") for c in range(M_BLOCKS)]
@@ -81,5 +81,5 @@ def tile_universalknowledgeintegrator_kernel(tc, table, w1x, w1k, know, b1, w2, 
             nc.tensor.matmul(total[:], w2_sb[:, c, :], g[:], start=(c == 0), stop=(c == M_BLOCKS - 1))
 
         result = held.tile([E, N], F32, name="result")
-        nc.scalar.activation(result[:], total[:], TANH, bias=shifts[:, M_BLOCKS:BIAS_ROWS])
+        nc.scalar.activation(result[:], total[:], TANH, bias=b2_sb[:, 0:1])
         nc.sync.dma_start(out, result[:])

@@ -34,8 +34,6 @@ def tile_universalknowledgeintegrator_kernel(tc, table, w1x, w1k, know, b1, w2, 
         nc.scalar.dma_start(w1x_sb[:], w1x)
         w2_sb = held.tile([P, M_BLOCKS, E], BF16, name="w2_sb")
         nc.scalar.dma_start(w2_sb[:], w2.rearrange("(c p) e -> p c e", p=P))
-        b2_sb = held.tile([E, 1], F32, name="b2_sb")
-        nc.sync.dma_start(b2_sb[:], b2)
 
         zeros = held.tile([P, P], BF16, name="zeros")
         nc.vector.memset(zeros[:], 0.0)
@@ -49,6 +47,8 @@ def tile_universalknowledgeintegrator_kernel(tc, table, w1x, w1k, know, b1, w2, 
 
         identity = held.tile([P, P], BF16, name="identity")
         make_identity(nc, identity[:])
+        b2_sb = held.tile([E, 1], F32, name="b2_sb")
+        nc.gpsimd.dma_start(b2_sb[:], b2)
         pick = held.tile([P, M_BLOCKS], F32, name="pick")
         nc.vector.tensor_copy(pick[:], identity[:, 0:M_BLOCKS])
         flipped = banks.tile([D, S], BF16, name="flipped")

@@ -5,7 +5,7 @@ P = 128
 S, D, M, E, N = 256, 128, 512, 128, 128
 S_BLOCKS = S // P
 M_BLOCKS = M // P
-WARM_MATMULS = 16
+WARM_MATMULS = 14
 FLOPS = 2 * D * M * N + 2 * D * M + 2 * M * E * N
 
 BF16, F32, U16 = mybir.dt.bfloat16, mybir.dt.float32, mybir.dt.uint16
@@ -19,15 +19,18 @@ def tile_universalknowledgeintegrator_kernel(tc, table, w1x, w1k, know, b1, w2, 
         tc.tile_pool(name="held", bufs=1) as held,
         tc.psum_pool(name="banks", bufs=1) as banks,
     ):
+        zeros = held.tile([P, P], BF16, name="zeros")
+        nc.vector.memset(zeros[:], 0.0)
+
         rows = held.tile([P, S_BLOCKS, D], BF16, name="rows")
         nc.sync.dma_start(rows[:], table.rearrange("(s p) d -> p s d", p=P))
         offsets = held.tile([P, N // 16], U16, name="offsets")
         nc.sync.dma_start(offsets[:], offs)
-        bias_rows = held.tile([P, P], F32, name="bias_rows")
-        nc.vector.memset(bias_rows[:], 0.0)
-        nc.scalar.dma_start(bias_rows[0:M_BLOCKS, :], b1.rearrange("(c p) o -> c (p o)", p=P))
         know_sb = held.tile([D, 1], BF16, name="know_sb")
         nc.scalar.dma_start(know_sb[:], know)
+        bias_rows = held.tile([P, P], F32, name="bias_rows")
+        nc.gpsimd.memset(bias_rows[:], 0.0)
+        nc.scalar.dma_start(bias_rows[0:M_BLOCKS, :], b1.rearrange("(c p) o -> c (p o)", p=P))
         w1k_sb = held.tile([D, M], BF16, name="w1k_sb")
         nc.sync.dma_start(w1k_sb[:], w1k)
         w1x_sb = held.tile([D, M], BF16, name="w1x_sb")
@@ -35,8 +38,6 @@ def tile_universalknowledgeintegrator_kernel(tc, table, w1x, w1k, know, b1, w2, 
         w2_sb = held.tile([P, M_BLOCKS, E], BF16, name="w2_sb")
         nc.scalar.dma_start(w2_sb[:], w2.rearrange("(c p) e -> p c e", p=P))
 
-        zeros = held.tile([P, P], BF16, name="zeros")
-        nc.vector.memset(zeros[:], 0.0)
         unread = banks.tile([P, P], F32, name="unread")
         for w in range(WARM_MATMULS):
             nc.tensor.matmul(unread[:], zeros[:], zeros[:], start=True, stop=True)
@@ -48,6 +49,7 @@ def tile_universalknowledgeintegrator_kernel(tc, table, w1x, w1k, know, b1, w2, 
         identity = held.tile([P, P], BF16, name="identity")
         make_identity(nc, identity[:])
         b2_sb = held.tile([E, 1], F32, name="b2_sb")
+        nc.vector.tensor_copy(b2_sb[:], identity[:, 0:1])
         nc.gpsimd.dma_start(b2_sb[:], b2)
         pick = held.tile([P, M_BLOCKS], F32, name="pick")
         nc.vector.tensor_copy(pick[:], identity[:, 0:M_BLOCKS])

@@ -4,6 +4,7 @@ from concourse.masks import make_identity
 P = 128
 S, D, M, E, N = 256, 128, 512, 128, 128
 S_BLOCKS = S // P
+ROWS = 64
 M_BLOCKS = M // P
 WARM_MATMULS = 14
 FLOPS = 2 * D * M * N + 2 * D * M + 2 * M * E * N
@@ -28,7 +29,7 @@ def tile_universalknowledgeintegrator_kernel(tc, table, w1x, w1k, know, b1, w2, 
         nc.sync.dma_start(offsets[:], offs)
         know_sb = held.tile([D, 1], BF16, name="know_sb")
         nc.scalar.dma_start(know_sb[:], know)
-        bias_rows = held.tile([P, P], F32, name="bias_rows")
+        bias_rows = held.tile([ROWS, P], F32, name="bias_rows")
         nc.gpsimd.memset(bias_rows[:], 0.0)
         nc.scalar.dma_start(bias_rows[0:M_BLOCKS, :], b1.rearrange("(c p) o -> c (p o)", p=P))
         w1k_sb = held.tile([D, M], BF16, name="w1k_sb")
@@ -51,23 +52,23 @@ def tile_universalknowledgeintegrator_kernel(tc, table, w1x, w1k, know, b1, w2, 
         b2_sb = held.tile([E, 1], F32, name="b2_sb")
         nc.vector.tensor_copy(b2_sb[:], identity[:, 0:1])
         nc.gpsimd.dma_start(b2_sb[:], b2)
-        pick = held.tile([P, M_BLOCKS], F32, name="pick")
-        nc.vector.tensor_copy(pick[:], identity[:, 0:M_BLOCKS])
+        identity_f32 = held.tile([ROWS, ROWS], F32, name="identity_f32")
+        nc.vector.tensor_copy(identity_f32[:], identity[0:ROWS, 0:ROWS])
         flipped = banks.tile([D, S], BF16, name="flipped")
         for s in range(S_BLOCKS):
             nc.tensor.transpose(flipped[:, s * P : (s + 1) * P], rows[:, s, :], identity[:])
         window = held.tile([D, S], BF16, name="window")
         nc.vector.tensor_copy(window[:], flipped[:])
 
-        shift_cols = banks.tile([P, M_BLOCKS], F32, name="shift_cols")
-        nc.tensor.matmul(shift_cols[:], bias_rows[:], pick[:], start=True, stop=False)
+        shift_cols = banks.tile([P, ROWS], F32, name="shift_cols")
+        nc.tensor.matmul(shift_cols[:], bias_rows[:], identity_f32[:], is_transpose=True, start=True, stop=False)
         for c in range(M_BLOCKS):
             nc.tensor.matmul(
                 shift_cols[:, c : c + 1], w1k_sb[:, c * P : (c + 1) * P], know_sb[:, 0:1],
                 start=False, stop=(c == M_BLOCKS - 1),
             )
         shifts = held.tile([P, M_BLOCKS], F32, name="shifts")
-        nc.vector.tensor_copy(shifts[:], shift_cols[:])
+        nc.vector.tensor_copy(shifts[:], shift_cols[:, 0:M_BLOCKS])
 
         pre = [banks.tile([P, N], F32, name=f"pre{c}") for c in range(M_BLOCKS)]
         for c in range(M_BLOCKS):

import concourse.mybir as mybir
from concourse.masks import make_identity

P = 128
S, D, M, E, N = 256, 128, 512, 128, 128
S_BLOCKS = S // P
ROWS = 64
M_BLOCKS = M // P
WARM_MATMULS = 14
FLOPS = 2 * D * M * N + 2 * D * M + 2 * M * E * N

BF16, F32, U16 = mybir.dt.bfloat16, mybir.dt.float32, mybir.dt.uint16
GELU = mybir.ActivationFunctionType.Gelu
TANH = mybir.ActivationFunctionType.Tanh


def tile_universalknowledgeintegrator_kernel(tc, table, w1x, w1k, know, b1, w2, b2, offs, out):
    nc = tc.nc
    with (
        tc.tile_pool(name="held", bufs=1) as held,
        tc.psum_pool(name="banks", bufs=1) as banks,
    ):
        zeros = held.tile([P, P], BF16, name="zeros")
        nc.vector.memset(zeros[:], 0.0)

        rows = held.tile([P, S_BLOCKS, D], BF16, name="rows")
        nc.sync.dma_start(rows[:], table.rearrange("(s p) d -> p s d", p=P))
        offsets = held.tile([P, N // 16], U16, name="offsets")
        nc.sync.dma_start(offsets[:], offs)
        know_sb = held.tile([D, 1], BF16, name="know_sb")
        nc.scalar.dma_start(know_sb[:], know)
        bias_rows = held.tile([ROWS, P], F32, name="bias_rows")
        nc.gpsimd.memset(bias_rows[:], 0.0)
        nc.scalar.dma_start(bias_rows[0:M_BLOCKS, :], b1.rearrange("(c p) o -> c (p o)", p=P))
        w1k_sb = held.tile([D, M], BF16, name="w1k_sb")
        nc.sync.dma_start(w1k_sb[:], w1k)
        w1x_sb = held.tile([D, M], BF16, name="w1x_sb")
        nc.scalar.dma_start(w1x_sb[:], w1x)
        w2_sb = held.tile([P, M_BLOCKS, E], BF16, name="w2_sb")
        nc.scalar.dma_start(w2_sb[:], w2.rearrange("(c p) e -> p c e", p=P))

        unread = banks.tile([P, P], F32, name="unread")
        for w in range(WARM_MATMULS):
            nc.tensor.matmul(unread[:], zeros[:], zeros[:], start=True, stop=True)

        warm = held.tile([P, 1], F32, name="warm")
        nc.vector.memset(warm[:], 0.0)
        nc.scalar.activation(warm[:], warm[:], GELU)

        identity = held.tile([P, P], BF16, name="identity")
        make_identity(nc, identity[:])
        b2_sb = held.tile([E, 1], F32, name="b2_sb")
        nc.vector.tensor_copy(b2_sb[:], identity[:, 0:1])
        nc.gpsimd.dma_start(b2_sb[:], b2)
        identity_f32 = held.tile([ROWS, ROWS], F32, name="identity_f32")
        nc.vector.tensor_copy(identity_f32[:], identity[0:ROWS, 0:ROWS])
        flipped = banks.tile([D, S], BF16, name="flipped")
        for s in range(S_BLOCKS):
            nc.tensor.transpose(flipped[:, s * P : (s + 1) * P], rows[:, s, :], identity[:])
        window = held.tile([D, S], BF16, name="window")
        nc.vector.tensor_copy(window[:], flipped[:])

        shift_cols = banks.tile([P, ROWS], F32, name="shift_cols")
        nc.tensor.matmul(shift_cols[:], bias_rows[:], identity_f32[:], is_transpose=True, start=True, stop=False)
        for c in range(M_BLOCKS):
            nc.tensor.matmul(
                shift_cols[:, c : c + 1], w1k_sb[:, c * P : (c + 1) * P], know_sb[:, 0:1],
                start=False, stop=(c == M_BLOCKS - 1),
            )
        shifts = held.tile([P, M_BLOCKS], F32, name="shifts")
        nc.vector.tensor_copy(shifts[:], shift_cols[:, 0:M_BLOCKS])

        pre = [banks.tile([P, N], F32, name=f"pre{c}") for c in range(M_BLOCKS)]
        for c in range(M_BLOCKS):
            nc.tensor.matmul(
                pre[c][:], w1x_sb[:, c * P : (c + 1) * P], window[:].indirect(offsets[:]),
                start=True, stop=True,
            )

        total = banks.tile([E, N], F32, name="total")
        for c in range(M_BLOCKS):
            g = held.tile([P, N], BF16, name=f"g{c}")
            nc.scalar.activation(g[:], pre[c][:], GELU, bias=shifts[:, c : c + 1])
            nc.tensor.matmul(total[:], w2_sb[:, c, :], g[:], start=(c == 0), stop=(c == M_BLOCKS - 1))

        result = held.tile([E, N], F32, name="result")
        nc.scalar.activation(result[:], total[:], TANH, bias=b2_sb[:, 0:1])
        nc.sync.dma_start(out, result[:])
